import numpy as np
import ml_dtypes


def mxq(x, axis, fmt="e4m3"):
    dtype, down = {"e4m3": (ml_dtypes.float8_e4m3fn, 7), "e5m2": (ml_dtypes.float8_e5m2, 14)}[fmt]
    v = np.moveaxis(np.asarray(x, np.float32).astype(ml_dtypes.bfloat16).astype(np.float64), axis, -1)
    blocks = v.reshape(v.shape[:-1] + (-1, 32))
    amax = np.abs(blocks).max(-1, keepdims=True)
    byte = np.maximum(np.where(amax > 0, np.frexp(amax)[1] - 1 + 127, 0) - down, 1)
    scale = np.exp2(byte - 127.0)
    codes = (blocks / scale).astype(np.float32).astype(dtype).astype(np.float64)
    return np.moveaxis((codes * scale).reshape(v.shape), -1, axis)


WIDE = False


def mx_kscale(k):
    if not WIDE:
        return np.ones(k)
    levels = np.array([10, -10, 5, -5, 0])
    if k % 512:
        return np.exp2(np.random.permutation(np.resize(levels, k // 32))).repeat(32)
    a = np.empty((k // 512, 16))
    for p in range(k // 512):
        a[p, :8] = np.random.permutation(np.resize(levels, 8))
        for g in range(8):
            far = levels[np.abs(levels - a[p, g]) >= 10]
            a[p, g + 8] = far[np.random.randint(len(far))]
    return np.exp2(a.ravel()).repeat(32)


BF16 = ml_dtypes.bfloat16


def bf(x):
    return np.asarray(x, np.float32).astype(BF16)


def f64(x):
    return np.asarray(x).astype(np.float64)


B, T, D, E, F = 4, 1024, 1024, 256, 4096
EPS = 1e-6


def rms_norm(x, w):
    rms = np.sqrt(np.mean(x * x, axis=-1, keepdims=True) + EPS)
    return x / rms * w


def setup_inputs():
    s = mx_kscale(D)
    return {"x": bf(np.random.standard_normal((B, T, D))),
            "attn_norm_w": bf((1.0 + 0.1 * np.random.standard_normal(D)) * s),
            "wq": bf(np.random.standard_normal((D, E)) * 1.5 / np.sqrt(D) / s[:, None]),
            "bq": bf(np.random.standard_normal(E) * 0.1),
            "wk": bf(np.random.standard_normal((D, E)) * 1.5 / np.sqrt(D) / s[:, None]),
            "bk": bf(np.random.standard_normal(E) * 0.1),
            "wv": bf(np.random.standard_normal((D, E)) / np.sqrt(D) / s[:, None]),
            "bv": bf(np.random.standard_normal(E) * 0.1)}


def reference(x, attn_norm_w, wq, bq, wk, bk, wv, bv):
    xn = mxq(rms_norm(f64(x), f64(attn_norm_w)), 2, "e4m3")
    q = (xn @ mxq(f64(wq), 0, "e4m3")) + f64(bq)
    k = (xn @ mxq(f64(wk), 0, "e4m3")) + f64(bk)
    v = (xn @ mxq(f64(wv), 0, "e4m3")) + f64(bv)
    return q, k, v

@@ -1,0 +1,281 @@
+from contextlib import ExitStack
+
+import concourse.mybir as mybir
+from concourse.masks import make_identity
+
+F32 = mybir.dt.float32
+BF16 = mybir.dt.bfloat16
+I32 = mybir.dt.int32
+U32 = mybir.dt.uint32
+U8 = mybir.dt.uint8
+FP8X4 = mybir.dt.float8_e4m3fn_x4
+ACT = mybir.ActivationFunctionType
+ALU = mybir.AluOpType
+
+P = 128
+PACK = 4
+PAIR = 2
+K_PASS = P * PACK
+TOKENS = 4 * 1024
+D = 1024
+E = 256
+PROJ = 3
+PASSES = D // K_PASS
+HALVES = D // (P * PAIR)
+TILES = 2
+UNIT = TILES * P
+UNITS = TOKENS // UNIT
+ALL_TILES = TOKENS // P
+BANK = 512
+PER_BANK = BANK // E
+OUT_BANKS = -(-PROJ // PER_BANK)
+LEAD = 4
+EPS = 1e-6
+GPSIMD_EVERY = 3
+
+FLOPS = 2 * TOKENS * D * PROJ * E
+
+
+def tile_tinyblock_pa_t_kernel(
+    tc, x, attn_norm_w, wq, bq, wk, bk, wv, bv, out_0, out_1, out_2
+):
+    nc = tc.nc
+    x_rows = x.flatten_outer_dims()
+    out_rows = [out_0.flatten_outer_dims(), out_1.flatten_outer_dims(), out_2.flatten_outer_dims()]
+    weights = [wq, wk, wv]
+    biases = [bq, bk, bv]
+
+    with ExitStack() as ctx:
+        ctx.enter_context(tc.manual_schedule())
+        const = ctx.enter_context(tc.tile_pool(name="const", bufs=1))
+        x_pool = ctx.enter_context(tc.tile_pool(name="x", bufs=UNITS))
+        small = ctx.enter_context(tc.tile_pool(name="small", bufs=LEAD + 2))
+        normed = ctx.enter_context(tc.tile_pool(name="normed", bufs=LEAD + 2))
+        work = ctx.enter_context(tc.tile_pool(name="work", bufs=3))
+        store = ctx.enter_context(tc.tile_pool(name="store", bufs=3))
+        psum_g = ctx.enter_context(tc.psum_pool(name="psum_g", bufs=1))
+        psum_t = ctx.enter_context(tc.psum_pool(name="psum_t", bufs=3))
+        psum_o = ctx.enter_context(tc.psum_pool(name="psum_o", bufs=2))
+
+        vector_row = const.tile([1, D + PROJ * E], BF16)
+        nc.sync.dma_start(out=vector_row[:, 0:D], in_=attn_norm_w.unsqueeze(0))
+        for i in range(PROJ):
+            nc.sync.dma_start(
+                out=vector_row[:, D + i * E : D + (i + 1) * E], in_=biases[i].unsqueeze(0)
+            )
+
+        w_raw = const.tile([P, PROJ, PASSES * PACK, E], BF16)
+
+        def load_weight(i):
+            nc.sync.dma_start(
+                out=w_raw[:, i].rearrange("p (c t) n -> p c (t n)", t=PACK),
+                in_=weights[i].rearrange("(c p t) n -> p c (t n)", p=P, t=PACK),
+            )
+
+        x_units = []
+
+        def load_unit(u):
+            x_unit = x_pool.tile([P, TILES, D], BF16, name="x_unit")
+            nc.sync.dma_start(
+                out=x_unit[:],
+                in_=x_rows[u * UNIT : (u + 1) * UNIT, :].rearrange("(p j) f -> p j f", j=TILES),
+            )
+            x_units.append(x_unit)
+
+        load_weight(0)
+        load_unit(0)
+        for i in range(1, PROJ):
+            load_weight(i)
+        for u in range(1, UNITS):
+            load_unit(u)
+
+        eps = const.tile([P, 1], F32)
+        nc.vector.memset(eps[:], EPS)
+        vectors = const.tile([P, D + PROJ * E], BF16)
+        nc.vector.memset(vectors[:].bitcast(I32), 0)
+        nc.vector.tensor_copy(out=vectors[0:1, :], in_=vector_row[:])
+        ones = const.tile([P, P], BF16)
+        nc.vector.memset(ones[:], 1.0)
+        ident = const.tile([P, P], F32)
+        make_identity(nc, ident[:])
+
+        warm = const.tile([P, 1], F32)
+        nc.scalar.activation(out=warm[:], in_=eps[:], func=ACT.Abs_reciprocal_sqrt)
+
+        gain_psum = psum_g.tile([P, D], BF16)
+        gain_sbuf = const.tile([P, D], BF16)
+        bias = const.tile([P, PROJ, E], F32)
+        for h in range(D // BANK):
+            nc.tensor.matmul(
+                out=gain_psum[:, h * BANK : (h + 1) * BANK], lhsT=ones[:],
+                rhs=vectors[:, h * BANK : (h + 1) * BANK], start=True, stop=True,
+            )
+        nc.scalar.copy(out=gain_sbuf[:], in_=gain_psum[:])
+        for i in range(PROJ):
+            spread = psum_t.tile([P, E], F32, tag="xt")
+            nc.tensor.matmul(
+                out=spread[:], lhsT=ones[:], rhs=vectors[:, D + i * E : D + (i + 1) * E],
+                start=True, stop=True,
+            )
+            nc.scalar.copy(out=bias[:, i, :], in_=spread[:])
+
+        w_grouped = const.tile([P, PROJ, PASSES, E, PACK], BF16, align_bytes=64)
+        w_codes = const.tile([P, PROJ, PASSES, E], U32, align_bytes=64)
+        w_scales = const.tile([P, PROJ, PASSES, E], U8, align_bytes=64)
+
+        def group_weight(i):
+            nc.vector.tensor_copy(
+                out=w_grouped[:, i],
+                in_=w_raw[:, i].rearrange("p (c t) n -> p c n t", t=PACK),
+            )
+
+        def quantise_weight(i):
+            nc.vector.quantize_mx(
+                out=w_codes[:, i].rearrange("p c n -> p (c n)").bitcast(FP8X4),
+                scales=w_scales[:, i].rearrange("p c n -> p (c n)"),
+                in_=w_grouped[:, i].rearrange("p c n t -> p (c n t)"),
+            )
+
+        group_weight(0)
+        for i in range(1, PROJ):
+            group_weight(i)
+            quantise_weight(i - 1)
+        quantise_weight(PROJ - 1)
+
+        sumsq_of = {}
+        rinv_of = {}
+        xn_of = {}
+        xt_of = {}
+        grouped_of = {}
+        codes_of = {}
+        scales_of = {}
+        acc_of = {}
+        result_of = {}
+
+        def statistics(n):
+            u, j = divmod(n, TILES)
+            if j == 0:
+                sumsq = small.tile([P, TILES], F32, name="sumsq")
+                sumsq_of[u] = sumsq
+            squares = work.tile([P, D], BF16, name="squares")
+            nc.scalar.activation(
+                out=squares[:], in_=x_units[u][:, j, :], func=ACT.Square,
+                accum_out=sumsq_of[u][:, j : j + 1],
+            )
+            if j == TILES - 1:
+                rinv = small.tile([P, TILES], F32, name="rinv")
+                nc.scalar.activation(
+                    out=rinv[:], in_=sumsq_of[u][:], func=ACT.Abs_reciprocal_sqrt,
+                    scale=1.0 / D, bias=eps[:],
+                )
+                rinv_of[u] = rinv
+
+        def normalise(n):
+            u, j = divmod(n, TILES)
+            rinv = rinv_of[u][:, j : j + 1]
+            xn = normed.tile([P, D], BF16, name="xn")
+            if n % GPSIMD_EVERY == GPSIMD_EVERY - 1:
+                scaled = work.tile([P, D], F32, name="scaled")
+                nc.gpsimd.tensor_scalar(
+                    out=scaled[:], in0=x_units[u][:, j, :], scalar1=rinv, scalar2=1.0,
+                    op0=ALU.mult, op1=ALU.mult,
+                )
+                nc.gpsimd.tensor_tensor(out=xn[:], in0=scaled[:], in1=gain_sbuf[:], op=ALU.mult)
+            else:
+                nc.vector.scalar_tensor_tensor(
+                    out=xn[:], in0=x_units[u][:, j, :], scalar=rinv, in1=gain_psum[:],
+                    op0=ALU.mult, op1=ALU.mult,
+                )
+            xn_of[n] = xn
+
+        def transpose(n):
+            xn_words = xn_of[n][:].bitcast(F32)
+            xt = psum_t.tile([P, HALVES, P], F32, name="xt")
+            for h in range(HALVES):
+                c, u = divmod(h, PAIR)
+                first = c * PAIR * P
+                nc.tensor.transpose(
+                    out=xt[:, h, :],
+                    in_=xn_words[:, first + u : first + PAIR * P : PAIR],
+                    identity=ident[:],
+                )
+            xt_of[n] = xt
+
+        def copy_out(n):
+            grouped = work.tile([P, PASSES, P, PACK], BF16, name="grouped", align_bytes=64)
+            nc.scalar.copy(
+                out=grouped[:]
+                .rearrange("p c r t -> p (c r t)")
+                .bitcast(F32)
+                .rearrange("p (c r u) -> p c r u", c=PASSES, u=PAIR),
+                in_=xt_of[n][:].rearrange("p (c u) r -> p c r u", u=PAIR),
+            )
+            grouped_of[n] = grouped
+
+        def quantise(n):
+            codes = work.tile([P, PASSES, P], U32, name="codes", align_bytes=64)
+            scales = work.tile([P, PASSES, P], U8, name="scales", align_bytes=64)
+            nc.vector.quantize_mx(
+                out=codes[:].rearrange("p c r -> p (c r)").bitcast(FP8X4),
+                scales=scales[:].rearrange("p c r -> p (c r)"),
+                in_=grouped_of[n][:].rearrange("p c r t -> p (c r t)"),
+            )
+            codes_of[n] = codes
+            scales_of[n] = scales
+
+        def project(n):
+            acc_of[n] = []
+            for b in range(OUT_BANKS):
+                acc = psum_o.tile([P, PER_BANK, E], F32, name="acc%d" % b)
+                acc_of[n].append(acc)
+            for i in range(PROJ):
+                for c in range(PASSES):
+                    nc.tensor.matmul_mx(
+                        out=acc_of[n][i // PER_BANK][:, i % PER_BANK, :],
+                        lhsT=codes_of[n][:, c, :].bitcast(FP8X4),
+                        lhsT_scale=scales_of[n][:, c, :],
+                        rhs=w_codes[:, i, c, :].bitcast(FP8X4),
+                        rhs_scale=w_scales[:, i, c, :],
+                        start=(c == 0),
+                        stop=(c == PASSES - 1),
+                    )
+
+        def add_bias_and_store(n):
+            u, j = divmod(n, TILES)
+            if j == 0:
+                result = store.tile([P, PROJ, TILES, E], F32, name="result")
+                result_of[u] = result
+            for b in range(OUT_BANKS):
+                first = b * PER_BANK
+                last = min(PROJ, first + PER_BANK)
+                nc.vector.tensor_tensor(
+                    out=result_of[u][:, first:last, j, :],
+                    in0=acc_of[n][b][:, 0 : last - first, :],
+                    in1=bias[:, first:last, :],
+                    op=ALU.add,
+                )
+            if j == TILES - 1:
+                for i in range(PROJ):
+                    nc.sync.dma_start(
+                        out=out_rows[i][u * UNIT : (u + 1) * UNIT, :].rearrange(
+                            "(p j) e -> p j e", j=TILES
+                        ),
+                        in_=result_of[u][:, i],
+                    )
+
+        for n in range(LEAD):
+            statistics(n)
+        for step in range(ALL_TILES + 3):
+            if 0 <= step - 1 < ALL_TILES:
+                copy_out(step - 1)
+            if step + LEAD < ALL_TILES:
+                statistics(step + LEAD)
+            if 0 <= step - 2 < ALL_TILES:
+                project(step - 2)
+            if step < ALL_TILES:
+                normalise(step)
+                transpose(step)
+            if 0 <= step - 3 < ALL_TILES:
+                add_bias_and_store(step - 3)
+            if 0 <= step - 1 < ALL_TILES:
+                quantise(step - 1)

@@ -20,20 +20,27 @@ TOKENS = 4 * 1024
 D = 1024
 E = 256
 PROJ = 3
+QK = 2
 PASSES = D // K_PASS
-HALVES = D // (P * PAIR)
 TILES = 2
 UNIT = TILES * P
 UNITS = TOKENS // UNIT
 ALL_TILES = TOKENS // P
 BANK = 512
-PER_BANK = BANK // E
-OUT_BANKS = -(-PROJ // PER_BANK)
-LEAD = 4
 EPS = 1e-6
-GPSIMD_EVERY = 3
+LEAD = 3
+HEAD_LEAD = 2
+LAG = 4
+GPSIMD_TURNS = (1, 3)
+GPSIMD_CYCLE = 5
+GPSIMD_FIRST = 5
+CHUNKS = 2
 
 FLOPS = 2 * TOKENS * D * PROJ * E
+
+
+def on_gpsimd(n):
+    return n >= GPSIMD_FIRST and n % GPSIMD_CYCLE in GPSIMD_TURNS
 
 
 def tile_tinyblock_pa_t_kernel(
@@ -49,51 +56,56 @@ def tile_tinyblock_pa_t_kernel(
         ctx.enter_context(tc.manual_schedule())
         const = ctx.enter_context(tc.tile_pool(name="const", bufs=1))
         x_pool = ctx.enter_context(tc.tile_pool(name="x", bufs=UNITS))
-        small = ctx.enter_context(tc.tile_pool(name="small", bufs=LEAD + 2))
-        normed = ctx.enter_context(tc.tile_pool(name="normed", bufs=LEAD + 2))
+        small = ctx.enter_context(tc.tile_pool(name="small", bufs=LEAD + 5))
+        squared = ctx.enter_context(tc.tile_pool(name="squared", bufs=2))
+        normed = ctx.enter_context(tc.tile_pool(name="normed", bufs=LEAD + 3))
         work = ctx.enter_context(tc.tile_pool(name="work", bufs=3))
+        coded = ctx.enter_context(tc.tile_pool(name="coded", bufs=LAG + 2))
         store = ctx.enter_context(tc.tile_pool(name="store", bufs=3))
         psum_g = ctx.enter_context(tc.psum_pool(name="psum_g", bufs=1))
-        psum_t = ctx.enter_context(tc.psum_pool(name="psum_t", bufs=3))
-        psum_o = ctx.enter_context(tc.psum_pool(name="psum_o", bufs=2))
+        psum_t = ctx.enter_context(tc.psum_pool(name="psum_t", bufs=2))
+        psum_o = ctx.enter_context(tc.psum_pool(name="psum_o", bufs=5))
 
-        vector_row = const.tile([1, D + PROJ * E], BF16)
-        nc.sync.dma_start(out=vector_row[:, 0:D], in_=attn_norm_w.unsqueeze(0))
-        for i in range(PROJ):
-            nc.sync.dma_start(
-                out=vector_row[:, D + i * E : D + (i + 1) * E], in_=biases[i].unsqueeze(0)
-            )
+        gain_row = const.tile([P, D], BF16)
+        nc.gpsimd.memset(gain_row[:].bitcast(I32), 0)
+        bias_row = const.tile([P, PROJ * E], BF16)
+        nc.gpsimd.memset(bias_row[:].bitcast(I32), 0)
+        nc.sync.dma_start(out=gain_row[0:1, :], in_=attn_norm_w.unsqueeze(0))
 
-        w_raw = const.tile([P, PROJ, PASSES * PACK, E], BF16)
+        w_raw = const.tile([P, PROJ, PASSES, PACK, E], BF16)
 
         def load_weight(i):
             nc.sync.dma_start(
-                out=w_raw[:, i].rearrange("p (c t) n -> p c (t n)", t=PACK),
+                out=w_raw[:, i].rearrange("p c t n -> p c (t n)"),
                 in_=weights[i].rearrange("(c p t) n -> p c (t n)", p=P, t=PACK),
             )
 
         x_units = []
 
-        def load_unit(u):
+        def load_unit(u, by_tile):
             x_unit = x_pool.tile([P, TILES, D], BF16, name="x_unit")
-            nc.sync.dma_start(
-                out=x_unit[:],
-                in_=x_rows[u * UNIT : (u + 1) * UNIT, :].rearrange("(p j) f -> p j f", j=TILES),
-            )
+            rows = x_rows[u * UNIT : (u + 1) * UNIT, :].rearrange("(p j) f -> p j f", j=TILES)
+            if by_tile:
+                for j in range(TILES):
+                    nc.sync.dma_start(out=x_unit[:, j, :], in_=rows[:, j, :])
+            else:
+                nc.sync.dma_start(out=x_unit[:], in_=rows)
             x_units.append(x_unit)
 
+        load_unit(0, True)
         load_weight(0)
-        load_unit(0)
+        load_unit(1, False)
+        for i in range(PROJ):
+            nc.sync.dma_start(
+                out=bias_row[0:1, i * E : (i + 1) * E], in_=biases[i].unsqueeze(0)
+            )
         for i in range(1, PROJ):
             load_weight(i)
-        for u in range(1, UNITS):
-            load_unit(u)
+        for u in range(2, UNITS):
+            load_unit(u, False)
 
         eps = const.tile([P, 1], F32)
         nc.vector.memset(eps[:], EPS)
-        vectors = const.tile([P, D + PROJ * E], BF16)
-        nc.vector.memset(vectors[:].bitcast(I32), 0)
-        nc.vector.tensor_copy(out=vectors[0:1, :], in_=vector_row[:])
         ones = const.tile([P, P], BF16)
         nc.vector.memset(ones[:], 1.0)
         ident = const.tile([P, P], F32)
@@ -104,43 +116,45 @@ def tile_tinyblock_pa_t_kernel(
 
         gain_psum = psum_g.tile([P, D], BF16)
         gain_sbuf = const.tile([P, D], BF16)
-        bias = const.tile([P, PROJ, E], F32)
         for h in range(D // BANK):
             nc.tensor.matmul(
                 out=gain_psum[:, h * BANK : (h + 1) * BANK], lhsT=ones[:],
-                rhs=vectors[:, h * BANK : (h + 1) * BANK], start=True, stop=True,
+                rhs=gain_row[:, h * BANK : (h + 1) * BANK], start=True, stop=True,
             )
-        nc.scalar.copy(out=gain_sbuf[:], in_=gain_psum[:])
-        for i in range(PROJ):
-            spread = psum_t.tile([P, E], F32, tag="xt")
+        nc.vector.tensor_copy(out=gain_sbuf[:], in_=gain_psum[:])
+        bias = const.tile([P, PROJ, E], F32)
+        bias_psum = []
+        for first, last in ((0, QK), (QK, PROJ)):
+            spread = psum_o.tile([P, QK, E], F32, tag="acc", name="spread")
             nc.tensor.matmul(
-                out=spread[:], lhsT=ones[:], rhs=vectors[:, D + i * E : D + (i + 1) * E],
-                start=True, stop=True,
+                out=spread[:, 0 : last - first, :].rearrange("p i n -> p (i n)"), lhsT=ones[:],
+                rhs=bias_row[:, first * E : last * E], start=True, stop=True,
             )
-            nc.scalar.copy(out=bias[:, i, :], in_=spread[:])
+            bias_psum.append((spread, first, last))
 
-        w_grouped = const.tile([P, PROJ, PASSES, E, PACK], BF16, align_bytes=64)
-        w_codes = const.tile([P, PROJ, PASSES, E], U32, align_bytes=64)
-        w_scales = const.tile([P, PROJ, PASSES, E], U8, align_bytes=64)
+        w_grouped = const.tile([P, PASSES, PROJ, E, PACK], BF16, align_bytes=64)
+        w_codes = const.tile([P, PASSES, PROJ, E], U32, align_bytes=64)
+        w_scales = const.tile([P, PASSES, PROJ, E], U8, align_bytes=64)
 
-        def group_weight(i):
+        def group_weight_on_vector(i):
             nc.vector.tensor_copy(
-                out=w_grouped[:, i],
-                in_=w_raw[:, i].rearrange("p (c t) n -> p c n t", t=PACK),
+                out=w_grouped[:, :, i], in_=w_raw[:, i].rearrange("p c t n -> p c n t")
             )
 
-        def quantise_weight(i):
-            nc.vector.quantize_mx(
-                out=w_codes[:, i].rearrange("p c n -> p (c n)").bitcast(FP8X4),
-                scales=w_scales[:, i].rearrange("p c n -> p (c n)"),
-                in_=w_grouped[:, i].rearrange("p c n t -> p (c n t)"),
-            )
+        def group_weight_on_gpsimd(i):
+            for c in range(PASSES):
+                nc.gpsimd.tensor_scalar(
+                    out=w_grouped[:, c, i], in0=w_raw[:, i, c].rearrange("p t n -> p n t"),
+                    scalar1=1.0, scalar2=0.0, op0=ALU.mult, op1=ALU.add,
+                )
 
-        group_weight(0)
-        for i in range(1, PROJ):
-            group_weight(i)
-            quantise_weight(i - 1)
-        quantise_weight(PROJ - 1)
+        def quantise_weights(first, last):
+            for c in range(PASSES):
+                nc.vector.quantize_mx(
+                    out=w_codes[:, c, first:last].rearrange("p i n -> p (i n)").bitcast(FP8X4),
+                    scales=w_scales[:, c, first:last].rearrange("p i n -> p (i n)"),
+                    in_=w_grouped[:, c, first:last].rearrange("p i n t -> p (i n t)"),
+                )
 
         sumsq_of = {}
         rinv_of = {}
@@ -152,53 +166,60 @@ def tile_tinyblock_pa_t_kernel(
         acc_of = {}
         result_of = {}
 
-        def statistics(n):
+        def square(n):
             u, j = divmod(n, TILES)
-            if j == 0:
-                sumsq = small.tile([P, TILES], F32, name="sumsq")
-                sumsq_of[u] = sumsq
-            squares = work.tile([P, D], BF16, name="squares")
+            sumsq = small.tile([P, 1], F32, name="sumsq")
+            squares = squared.tile([P, D], BF16, name="squares")
             nc.scalar.activation(
-                out=squares[:], in_=x_units[u][:, j, :], func=ACT.Square,
-                accum_out=sumsq_of[u][:, j : j + 1],
+                out=squares[:], in_=x_units[u][:, j, :], func=ACT.Square, accum_out=sumsq[:]
             )
-            if j == TILES - 1:
-                rinv = small.tile([P, TILES], F32, name="rinv")
-                nc.scalar.activation(
-                    out=rinv[:], in_=sumsq_of[u][:], func=ACT.Abs_reciprocal_sqrt,
-                    scale=1.0 / D, bias=eps[:],
-                )
-                rinv_of[u] = rinv
+            sumsq_of[n] = sumsq
 
-        def normalise(n):
+        def invert(n):
+            rinv = small.tile([P, 1], F32, name="rinv")
+            nc.scalar.activation(
+                out=rinv[:], in_=sumsq_of[n][:], func=ACT.Abs_reciprocal_sqrt,
+                scale=1.0 / D, bias=eps[:],
+            )
+            rinv_of[n] = rinv
+
+        def normalise_on_gpsimd(n):
             u, j = divmod(n, TILES)
-            rinv = rinv_of[u][:, j : j + 1]
             xn = normed.tile([P, D], BF16, name="xn")
-            if n % GPSIMD_EVERY == GPSIMD_EVERY - 1:
-                scaled = work.tile([P, D], F32, name="scaled")
+            scaled = work.tile([P, D], F32, name="scaled")
+            width = D // CHUNKS
+            for h in range(CHUNKS):
+                cols = slice(h * width, (h + 1) * width)
                 nc.gpsimd.tensor_scalar(
-                    out=scaled[:], in0=x_units[u][:, j, :], scalar1=rinv, scalar2=1.0,
-                    op0=ALU.mult, op1=ALU.mult,
+                    out=scaled[:, cols], in0=x_units[u][:, j, cols], scalar1=rinv_of[n][:],
+                    scalar2=1.0, op0=ALU.mult, op1=ALU.mult,
                 )
-                nc.gpsimd.tensor_tensor(out=xn[:], in0=scaled[:], in1=gain_sbuf[:], op=ALU.mult)
-            else:
-                nc.vector.scalar_tensor_tensor(
-                    out=xn[:], in0=x_units[u][:, j, :], scalar=rinv, in1=gain_psum[:],
-                    op0=ALU.mult, op1=ALU.mult,
+            for h in range(CHUNKS):
+                cols = slice(h * width, (h + 1) * width)
+                nc.gpsimd.tensor_tensor(
+                    out=xn[:, cols], in0=scaled[:, cols], in1=gain_sbuf[:, cols], op=ALU.mult
                 )
+            xn_of[n] = xn
+
+        def normalise_on_vector(n):
+            u, j = divmod(n, TILES)
+            xn = normed.tile([P, D], BF16, name="xn")
+            nc.vector.scalar_tensor_tensor(
+                out=xn[:], in0=x_units[u][:, j, :], scalar=rinv_of[n][:], in1=gain_psum[:],
+                op0=ALU.mult, op1=ALU.mult,
+            )
             xn_of[n] = xn
 
         def transpose(n):
             xn_words = xn_of[n][:].bitcast(F32)
-            xt = psum_t.tile([P, HALVES, P], F32, name="xt")
-            for h in range(HALVES):
-                c, u = divmod(h, PAIR)
-                first = c * PAIR * P
-                nc.tensor.transpose(
-                    out=xt[:, h, :],
-                    in_=xn_words[:, first + u : first + PAIR * P : PAIR],
-                    identity=ident[:],
-                )
+            xt = psum_t.tile([P, PASSES, PAIR, P], F32, name="xt")
+            for c in range(PASSES):
+                for u in range(PAIR):
+                    nc.tensor.transpose(
+                        out=xt[:, c, u, :],
+                        in_=xn_words[:, c * PAIR * P + u : (c + 1) * PAIR * P : PAIR],
+                        identity=ident[:],
+                    )
             xt_of[n] = xt
 
         def copy_out(n):
@@ -208,13 +229,13 @@ def tile_tinyblock_pa_t_kernel(
                 .rearrange("p c r t -> p (c r t)")
                 .bitcast(F32)
                 .rearrange("p (c r u) -> p c r u", c=PASSES, u=PAIR),
-                in_=xt_of[n][:].rearrange("p (c u) r -> p c r u", u=PAIR),
+                in_=xt_of[n][:].rearrange("p c u r -> p c r u"),
             )
             grouped_of[n] = grouped
 
         def quantise(n):
-            codes = work.tile([P, PASSES, P], U32, name="codes", align_bytes=64)
-            scales = work.tile([P, PASSES, P], U8, name="scales", align_bytes=64)
+            codes = coded.tile([P, PASSES, P], U32, name="codes", align_bytes=64)
+            scales = coded.tile([P, PASSES, P], U8, name="scales", align_bytes=64)
             nc.vector.quantize_mx(
                 out=codes[:].rearrange("p c r -> p (c r)").bitcast(FP8X4),
                 scales=scales[:].rearrange("p c r -> p (c r)"),
@@ -223,59 +244,83 @@ def tile_tinyblock_pa_t_kernel(
             codes_of[n] = codes
             scales_of[n] = scales
 
+        def passes(n, out, first, last):
+            for c in range(PASSES):
+                nc.tensor.matmul_mx(
+                    out=out,
+                    lhsT=codes_of[n][:, c, :].bitcast(FP8X4),
+                    lhsT_scale=scales_of[n][:, c, :],
+                    rhs=w_codes[:, c, first:last].rearrange("p i n -> p (i n)").bitcast(FP8X4),
+                    rhs_scale=w_scales[:, c, first:last].rearrange("p i n -> p (i n)"),
+                    start=(c == 0),
+                    stop=(c == PASSES - 1),
+                )
+
         def project(n):
-            acc_of[n] = []
-            for b in range(OUT_BANKS):
-                acc = psum_o.tile([P, PER_BANK, E], F32, name="acc%d" % b)
-                acc_of[n].append(acc)
-            for i in range(PROJ):
-                for c in range(PASSES):
-                    nc.tensor.matmul_mx(
-                        out=acc_of[n][i // PER_BANK][:, i % PER_BANK, :],
-                        lhsT=codes_of[n][:, c, :].bitcast(FP8X4),
-                        lhsT_scale=scales_of[n][:, c, :],
-                        rhs=w_codes[:, i, c, :].bitcast(FP8X4),
-                        rhs_scale=w_scales[:, i, c, :],
-                        start=(c == 0),
-                        stop=(c == PASSES - 1),
-                    )
+            u, j = divmod(n, TILES)
+            acc = psum_o.tile([P, QK, E], F32, tag="acc", name="acc")
+            acc_of[n] = acc
+            passes(n, acc[:].rearrange("p i n -> p (i n)"), 0, QK)
+            if j == 0:
+                acc_v = psum_o.tile([P, TILES, E], F32, tag="acc", name="acc_v")
+                acc_of[u, "v"] = acc_v
+            passes(n, acc_of[u, "v"][:, j, :], QK, PROJ)
+
+        def store_projection(u, i):
+            nc.sync.dma_start(
+                out=out_rows[i][u * UNIT : (u + 1) * UNIT, :].rearrange("(p j) e -> p j e", j=TILES),
+                in_=result_of[u][:, i],
+            )
 
         def add_bias_and_store(n):
             u, j = divmod(n, TILES)
             if j == 0:
                 result = store.tile([P, PROJ, TILES, E], F32, name="result")
                 result_of[u] = result
-            for b in range(OUT_BANKS):
-                first = b * PER_BANK
-                last = min(PROJ, first + PER_BANK)
-                nc.vector.tensor_tensor(
-                    out=result_of[u][:, first:last, j, :],
-                    in0=acc_of[n][b][:, 0 : last - first, :],
-                    in1=bias[:, first:last, :],
-                    op=ALU.add,
-                )
+            nc.vector.tensor_tensor(
+                out=result_of[u][:, 0:QK, j, :], in0=acc_of[n][:], in1=bias[:, 0:QK, :], op=ALU.add
+            )
             if j == TILES - 1:
-                for i in range(PROJ):
-                    nc.sync.dma_start(
-                        out=out_rows[i][u * UNIT : (u + 1) * UNIT, :].rearrange(
-                            "(p j) e -> p j e", j=TILES
-                        ),
-                        in_=result_of[u][:, i],
-                    )
+                for i in range(QK):
+                    store_projection(u, i)
+                nc.vector.tensor_tensor(
+                    out=result_of[u][:, QK], in0=acc_of[u, "v"][:],
+                    in1=bias[:, QK:PROJ, :].to_broadcast([P, TILES, E]), op=ALU.add,
+                )
+                store_projection(u, QK)
 
-        for n in range(LEAD):
-            statistics(n)
-        for step in range(ALL_TILES + 3):
+        square(0)
+        invert(0)
+        square(1)
+        invert(1)
+        group_weight_on_gpsimd(0)
+        group_weight_on_gpsimd(1)
+        for step in range(ALL_TILES + LAG + 1):
             if 0 <= step - 1 < ALL_TILES:
                 copy_out(step - 1)
-            if step + LEAD < ALL_TILES:
-                statistics(step + LEAD)
-            if 0 <= step - 2 < ALL_TILES:
-                project(step - 2)
+            lead = HEAD_LEAD if step < LAG - 1 else LEAD
+            while len(rinv_of) <= min(ALL_TILES - 1, step + lead):
+                n = len(rinv_of)
+                square(n)
+                invert(n)
+                if on_gpsimd(n):
+                    normalise_on_gpsimd(n)
+            if step == 2:
+                for spread, first, last in bias_psum:
+                    nc.scalar.copy(out=bias[:, first:last, :], in_=spread[:, 0 : last - first, :])
+            if 0 <= step - LAG < ALL_TILES:
+                project(step - LAG)
             if step < ALL_TILES:
-                normalise(step)
+                if not on_gpsimd(step):
+                    normalise_on_vector(step)
                 transpose(step)
-            if 0 <= step - 3 < ALL_TILES:
-                add_bias_and_store(step - 3)
+            if step == 1:
+                group_weight_on_vector(2)
+            if step == 2:
+                quantise_weights(0, QK)
+            if 0 <= step - LAG - 1 < ALL_TILES:
+                add_bias_and_store(step - LAG - 1)
             if 0 <= step - 1 < ALL_TILES:
                 quantise(step - 1)
+            if step == 3:
+                quantise_weights(QK, PROJ)

@@ -31,16 +31,14 @@ EPS = 1e-6
 LEAD = 3
 HEAD_LEAD = 2
 LAG = 4
-GPSIMD_TURNS = (1, 3)
-GPSIMD_CYCLE = 5
-GPSIMD_FIRST = 5
-CHUNKS = 2
+GPSIMD_COLS = 320
+GPSIMD_FIRST = 4
 
 FLOPS = 2 * TOKENS * D * PROJ * E
 
 
-def on_gpsimd(n):
-    return n >= GPSIMD_FIRST and n % GPSIMD_CYCLE in GPSIMD_TURNS
+def vector_cols(n):
+    return D - GPSIMD_COLS if n >= GPSIMD_FIRST else D
 
 
 def tile_tinyblock_pa_t_kernel(
@@ -59,7 +57,7 @@ def tile_tinyblock_pa_t_kernel(
         small = ctx.enter_context(tc.tile_pool(name="small", bufs=LEAD + 5))
         squared = ctx.enter_context(tc.tile_pool(name="squared", bufs=2))
         normed = ctx.enter_context(tc.tile_pool(name="normed", bufs=LEAD + 3))
-        work = ctx.enter_context(tc.tile_pool(name="work", bufs=3))
+        work = ctx.enter_context(tc.tile_pool(name="work", bufs=4))
         coded = ctx.enter_context(tc.tile_pool(name="coded", bufs=LAG + 2))
         store = ctx.enter_context(tc.tile_pool(name="store", bufs=3))
         psum_g = ctx.enter_context(tc.psum_pool(name="psum_g", bufs=1))
@@ -183,32 +181,28 @@ def tile_tinyblock_pa_t_kernel(
             )
             rinv_of[n] = rinv
 
-        def normalise_on_gpsimd(n):
+        def normalise_on_gpsimd(n, scratch):
             u, j = divmod(n, TILES)
             xn = normed.tile([P, D], BF16, name="xn")
-            scaled = work.tile([P, D], F32, name="scaled")
-            width = D // CHUNKS
-            for h in range(CHUNKS):
-                cols = slice(h * width, (h + 1) * width)
+            xn_of[n] = xn
+            if vector_cols(n) < D:
+                cols = slice(vector_cols(n), D)
+                scaled = scratch[:].rearrange("p c r t -> p (c r t)").bitcast(F32)[:, 0:GPSIMD_COLS]
                 nc.gpsimd.tensor_scalar(
-                    out=scaled[:, cols], in0=x_units[u][:, j, cols], scalar1=rinv_of[n][:],
+                    out=scaled, in0=x_units[u][:, j, cols], scalar1=rinv_of[n][:],
                     scalar2=1.0, op0=ALU.mult, op1=ALU.mult,
                 )
-            for h in range(CHUNKS):
-                cols = slice(h * width, (h + 1) * width)
                 nc.gpsimd.tensor_tensor(
-                    out=xn[:, cols], in0=scaled[:, cols], in1=gain_sbuf[:, cols], op=ALU.mult
+                    out=xn[:, cols], in0=scaled, in1=gain_sbuf[:, cols], op=ALU.mult
                 )
-            xn_of[n] = xn
 
         def normalise_on_vector(n):
             u, j = divmod(n, TILES)
-            xn = normed.tile([P, D], BF16, name="xn")
+            cols = slice(0, vector_cols(n))
             nc.vector.scalar_tensor_tensor(
-                out=xn[:], in0=x_units[u][:, j, :], scalar=rinv_of[n][:], in1=gain_psum[:],
-                op0=ALU.mult, op1=ALU.mult,
+                out=xn_of[n][:, cols], in0=x_units[u][:, j, cols], scalar=rinv_of[n][:],
+                in1=gain_psum[:, cols], op0=ALU.mult, op1=ALU.mult,
             )
-            xn_of[n] = xn
 
         def transpose(n):
             xn_words = xn_of[n][:].bitcast(F32)
@@ -303,16 +297,15 @@ def tile_tinyblock_pa_t_kernel(
                 n = len(rinv_of)
                 square(n)
                 invert(n)
-                if on_gpsimd(n):
-                    normalise_on_gpsimd(n)
             if step == 2:
                 for spread, first, last in bias_psum:
                     nc.scalar.copy(out=bias[:, first:last, :], in_=spread[:, 0 : last - first, :])
             if 0 <= step - LAG < ALL_TILES:
                 project(step - LAG)
             if step < ALL_TILES:
-                if not on_gpsimd(step):
-                    normalise_on_vector(step)
+                if step < GPSIMD_FIRST:
+                    normalise_on_gpsimd(step, None)
+                normalise_on_vector(step)
                 transpose(step)
             if step == 1:
                 group_weight_on_vector(2)
@@ -322,5 +315,7 @@ def tile_tinyblock_pa_t_kernel(
                 add_bias_and_store(step - LAG - 1)
             if 0 <= step - 1 < ALL_TILES:
                 quantise(step - 1)
+            if GPSIMD_FIRST <= step + 2 < ALL_TILES:
+                normalise_on_gpsimd(step + 2, grouped_of[step - 1])
             if step == 3:
                 quantise_weights(QK, PROJ)

@@ -29,16 +29,15 @@ ALL_TILES = TOKENS // P
 BANK = 512
 EPS = 1e-6
 LEAD = 3
-HEAD_LEAD = 2
-LAG = 4
+LAG = 2
 GPSIMD_COLS = 320
-GPSIMD_FIRST = 4
+GPSIMD_FIRST = 5
 
 FLOPS = 2 * TOKENS * D * PROJ * E
 
 
-def vector_cols(n):
-    return D - GPSIMD_COLS if n >= GPSIMD_FIRST else D
+def vector_cols(u):
+    return D - GPSIMD_COLS if u >= GPSIMD_FIRST else D
 
 
 def tile_tinyblock_pa_t_kernel(
@@ -54,11 +53,11 @@ def tile_tinyblock_pa_t_kernel(
         ctx.enter_context(tc.manual_schedule())
         const = ctx.enter_context(tc.tile_pool(name="const", bufs=1))
         x_pool = ctx.enter_context(tc.tile_pool(name="x", bufs=UNITS))
-        small = ctx.enter_context(tc.tile_pool(name="small", bufs=LEAD + 5))
+        small = ctx.enter_context(tc.tile_pool(name="small", bufs=LEAD + 3))
         squared = ctx.enter_context(tc.tile_pool(name="squared", bufs=2))
-        normed = ctx.enter_context(tc.tile_pool(name="normed", bufs=LEAD + 3))
-        work = ctx.enter_context(tc.tile_pool(name="work", bufs=4))
-        coded = ctx.enter_context(tc.tile_pool(name="coded", bufs=LAG + 2))
+        normed = ctx.enter_context(tc.tile_pool(name="normed", bufs=4))
+        work = ctx.enter_context(tc.tile_pool(name="work", bufs=3))
+        coded = ctx.enter_context(tc.tile_pool(name="coded", bufs=LAG + 1))
         store = ctx.enter_context(tc.tile_pool(name="store", bufs=3))
         psum_g = ctx.enter_context(tc.psum_pool(name="psum_g", bufs=1))
         psum_t = ctx.enter_context(tc.psum_pool(name="psum_t", bufs=2))
@@ -120,7 +119,7 @@ def tile_tinyblock_pa_t_kernel(
                 rhs=gain_row[:, h * BANK : (h + 1) * BANK], start=True, stop=True,
             )
         nc.vector.tensor_copy(out=gain_sbuf[:], in_=gain_psum[:])
-        bias = const.tile([P, PROJ, E], F32)
+        bias = const.tile([P, QK + TILES, E], F32)
         bias_psum = []
         for first, last in ((0, QK), (QK, PROJ)):
             spread = psum_o.tile([P, QK, E], F32, tag="acc", name="spread")
@@ -162,160 +161,170 @@ def tile_tinyblock_pa_t_kernel(
         codes_of = {}
         scales_of = {}
         acc_of = {}
-        result_of = {}
 
-        def square(n):
-            u, j = divmod(n, TILES)
-            sumsq = small.tile([P, 1], F32, name="sumsq")
+        def square(u, j):
+            if j == 0:
+                sumsq = small.tile([P, TILES], F32, name="sumsq")
+                sumsq_of[u] = sumsq
+                rinv = small.tile([P, TILES], F32, name="rinv")
+                rinv_of[u] = rinv
             squares = squared.tile([P, D], BF16, name="squares")
             nc.scalar.activation(
-                out=squares[:], in_=x_units[u][:, j, :], func=ACT.Square, accum_out=sumsq[:]
+                out=squares[:], in_=x_units[u][:, j, :], func=ACT.Square,
+                accum_out=sumsq_of[u][:, j : j + 1],
             )
-            sumsq_of[n] = sumsq
 
-        def invert(n):
-            rinv = small.tile([P, 1], F32, name="rinv")
+        def invert(u, first, last):
             nc.scalar.activation(
-                out=rinv[:], in_=sumsq_of[n][:], func=ACT.Abs_reciprocal_sqrt,
-                scale=1.0 / D, bias=eps[:],
+                out=rinv_of[u][:, first:last], in_=sumsq_of[u][:, first:last],
+                func=ACT.Abs_reciprocal_sqrt, scale=1.0 / D, bias=eps[:],
             )
-            rinv_of[n] = rinv
 
-        def normalise_on_gpsimd(n, scratch):
-            u, j = divmod(n, TILES)
-            xn = normed.tile([P, D], BF16, name="xn")
-            xn_of[n] = xn
-            if vector_cols(n) < D:
-                cols = slice(vector_cols(n), D)
-                scaled = scratch[:].rearrange("p c r t -> p (c r t)").bitcast(F32)[:, 0:GPSIMD_COLS]
+        def normalise_on_gpsimd(u, scratch):
+            cols = slice(vector_cols(u), D)
+            scaled = (
+                scratch[:].rearrange("p j c r t -> p (j c r t)").bitcast(F32)
+                [:, 0 : TILES * GPSIMD_COLS].rearrange("p (j m) -> p j m", j=TILES)
+            )
+            for j in range(TILES):
                 nc.gpsimd.tensor_scalar(
-                    out=scaled, in0=x_units[u][:, j, cols], scalar1=rinv_of[n][:],
+                    out=scaled[:, j], in0=x_units[u][:, j, cols], scalar1=rinv_of[u][:, j : j + 1],
                     scalar2=1.0, op0=ALU.mult, op1=ALU.mult,
                 )
-                nc.gpsimd.tensor_tensor(
-                    out=xn[:, cols], in0=scaled, in1=gain_sbuf[:, cols], op=ALU.mult
-                )
-
-        def normalise_on_vector(n):
-            u, j = divmod(n, TILES)
-            cols = slice(0, vector_cols(n))
-            nc.vector.scalar_tensor_tensor(
-                out=xn_of[n][:, cols], in0=x_units[u][:, j, cols], scalar=rinv_of[n][:],
-                in1=gain_psum[:, cols], op0=ALU.mult, op1=ALU.mult,
+            nc.gpsimd.tensor_tensor(
+                out=xn_of[u][:, :, cols], in0=scaled,
+                in1=gain_sbuf[:, cols].unsqueeze(1).to_broadcast([P, TILES, GPSIMD_COLS]),
+                op=ALU.mult,
             )
 
-        def transpose(n):
-            xn_words = xn_of[n][:].bitcast(F32)
+        def normalise_on_vector(u, j):
+            cols = slice(0, vector_cols(u))
+            nc.vector.scalar_tensor_tensor(
+                out=xn_of[u][:, j, cols], in0=x_units[u][:, j, cols],
+                scalar=rinv_of[u][:, j : j + 1], in1=gain_psum[:, cols],
+                op0=ALU.mult, op1=ALU.mult,
+            )
+
+        def transpose(u, j):
+            xn_words = xn_of[u][:, j, :].bitcast(F32)
             xt = psum_t.tile([P, PASSES, PAIR, P], F32, name="xt")
             for c in range(PASSES):
-                for u in range(PAIR):
+                for h in range(PAIR):
                     nc.tensor.transpose(
-                        out=xt[:, c, u, :],
-                        in_=xn_words[:, c * PAIR * P + u : (c + 1) * PAIR * P : PAIR],
+                        out=xt[:, c, h, :],
+                        in_=xn_words[:, c * PAIR * P + h : (c + 1) * PAIR * P : PAIR],
                         identity=ident[:],
                     )
-            xt_of[n] = xt
+            xt_of[u, j] = xt
 
-        def copy_out(n):
-            grouped = work.tile([P, PASSES, P, PACK], BF16, name="grouped", align_bytes=64)
+        def copy_out(u, j):
+            if j == 0:
+                grouped = work.tile(
+                    [P, TILES, PASSES, P, PACK], BF16, name="grouped", align_bytes=64
+                )
+                grouped_of[u] = grouped
             nc.scalar.copy(
-                out=grouped[:]
+                out=grouped_of[u][:, j]
                 .rearrange("p c r t -> p (c r t)")
                 .bitcast(F32)
-                .rearrange("p (c r u) -> p c r u", c=PASSES, u=PAIR),
-                in_=xt_of[n][:].rearrange("p c u r -> p c r u"),
+                .rearrange("p (c r h) -> p c r h", c=PASSES, h=PAIR),
+                in_=xt_of[u, j][:].rearrange("p c h r -> p c r h"),
             )
-            grouped_of[n] = grouped
 
-        def quantise(n):
-            codes = coded.tile([P, PASSES, P], U32, name="codes", align_bytes=64)
-            scales = coded.tile([P, PASSES, P], U8, name="scales", align_bytes=64)
+        def quantise(u):
+            codes = coded.tile([P, TILES, PASSES, P], U32, name="codes", align_bytes=64)
+            scales = coded.tile([P, TILES, PASSES, P], U8, name="scales", align_bytes=64)
             nc.vector.quantize_mx(
-                out=codes[:].rearrange("p c r -> p (c r)").bitcast(FP8X4),
-                scales=scales[:].rearrange("p c r -> p (c r)"),
-                in_=grouped_of[n][:].rearrange("p c r t -> p (c r t)"),
+                out=codes[:].rearrange("p j c r -> p (j c r)").bitcast(FP8X4),
+                scales=scales[:].rearrange("p j c r -> p (j c r)"),
+                in_=grouped_of[u][:].rearrange("p j c r t -> p (j c r t)"),
             )
-            codes_of[n] = codes
-            scales_of[n] = scales
+            codes_of[u] = codes
+            scales_of[u] = scales
 
-        def passes(n, out, first, last):
+        def passes(u, j, out, first, last):
             for c in range(PASSES):
                 nc.tensor.matmul_mx(
                     out=out,
-                    lhsT=codes_of[n][:, c, :].bitcast(FP8X4),
-                    lhsT_scale=scales_of[n][:, c, :],
+                    lhsT=codes_of[u][:, j, c, :].bitcast(FP8X4),
+                    lhsT_scale=scales_of[u][:, j, c, :],
                     rhs=w_codes[:, c, first:last].rearrange("p i n -> p (i n)").bitcast(FP8X4),
                     rhs_scale=w_scales[:, c, first:last].rearrange("p i n -> p (i n)"),
                     start=(c == 0),
                     stop=(c == PASSES - 1),
                 )
 
-        def project(n):
-            u, j = divmod(n, TILES)
+        def project(u, j):
             acc = psum_o.tile([P, QK, E], F32, tag="acc", name="acc")
-            acc_of[n] = acc
-            passes(n, acc[:].rearrange("p i n -> p (i n)"), 0, QK)
+            acc_of[u, j] = acc
+            passes(u, j, acc[:].rearrange("p i n -> p (i n)"), 0, QK)
             if j == 0:
                 acc_v = psum_o.tile([P, TILES, E], F32, tag="acc", name="acc_v")
                 acc_of[u, "v"] = acc_v
-            passes(n, acc_of[u, "v"][:, j, :], QK, PROJ)
+            passes(u, j, acc_of[u, "v"][:, j, :], QK, PROJ)
 
-        def store_projection(u, i):
-            nc.sync.dma_start(
-                out=out_rows[i][u * UNIT : (u + 1) * UNIT, :].rearrange("(p j) e -> p j e", j=TILES),
-                in_=result_of[u][:, i],
-            )
-
-        def add_bias_and_store(n):
-            u, j = divmod(n, TILES)
-            if j == 0:
-                result = store.tile([P, PROJ, TILES, E], F32, name="result")
-                result_of[u] = result
-            nc.vector.tensor_tensor(
-                out=result_of[u][:, 0:QK, j, :], in0=acc_of[n][:], in1=bias[:, 0:QK, :], op=ALU.add
-            )
-            if j == TILES - 1:
-                for i in range(QK):
-                    store_projection(u, i)
+        def add_bias_and_store(u):
+            result = store.tile([P, PROJ, TILES, E], F32, name="result")
+            for j in range(TILES):
                 nc.vector.tensor_tensor(
-                    out=result_of[u][:, QK], in0=acc_of[u, "v"][:],
-                    in1=bias[:, QK:PROJ, :].to_broadcast([P, TILES, E]), op=ALU.add,
+                    out=result[:, 0:QK, j, :], in0=acc_of[u, j][:], in1=bias[:, 0:QK, :],
+                    op=ALU.add,
                 )
-                store_projection(u, QK)
+            nc.vector.tensor_tensor(
+                out=result[:, QK], in0=acc_of[u, "v"][:], in1=bias[:, QK:, :], op=ALU.add
+            )
+            for i in range(PROJ):
+                nc.sync.dma_start(
+                    out=out_rows[i][u * UNIT : (u + 1) * UNIT, :].rearrange(
+                        "(p j) e -> p j e", j=TILES
+                    ),
+                    in_=result[:, i],
+                )
 
-        square(0)
-        invert(0)
-        square(1)
-        invert(1)
         group_weight_on_gpsimd(0)
         group_weight_on_gpsimd(1)
-        for step in range(ALL_TILES + LAG + 1):
-            if 0 <= step - 1 < ALL_TILES:
-                copy_out(step - 1)
-            lead = HEAD_LEAD if step < LAG - 1 else LEAD
-            while len(rinv_of) <= min(ALL_TILES - 1, step + lead):
-                n = len(rinv_of)
-                square(n)
-                invert(n)
-            if step == 2:
+        for j in range(TILES):
+            square(0, j)
+            invert(0, j, j + 1)
+        known = 1
+        for step in range(UNITS + LAG):
+            wanted = min(UNITS, step + (2 if step < 2 else 3 if step == 2 else LEAD + 1))
+            todo = list(range(known, wanted))
+            known = wanted
+            if step < UNITS:
+                if step < GPSIMD_FIRST:
+                    xn = normed.tile([P, TILES, D], BF16, name="xn")
+                    xn_of[step] = xn
+            for j in range(TILES):
+                if step < UNITS:
+                    normalise_on_vector(step, j)
+                if 0 <= step - LAG:
+                    project(step - LAG, j)
+                if step < UNITS:
+                    transpose(step, j)
+                for u in todo[0:1]:
+                    square(u, j)
+                if step < UNITS:
+                    copy_out(step, j)
+            for i, u in enumerate(todo):
+                if i > 0:
+                    for j in range(TILES):
+                        square(u, j)
+                invert(u, 0, TILES)
+            if step == 0:
+                group_weight_on_vector(2)
                 for spread, first, last in bias_psum:
                     nc.scalar.copy(out=bias[:, first:last, :], in_=spread[:, 0 : last - first, :])
-            if 0 <= step - LAG < ALL_TILES:
-                project(step - LAG)
-            if step < ALL_TILES:
-                if step < GPSIMD_FIRST:
-                    normalise_on_gpsimd(step, None)
-                normalise_on_vector(step)
-                transpose(step)
-            if step == 1:
-                group_weight_on_vector(2)
-            if step == 2:
-                quantise_weights(0, QK)
-            if 0 <= step - LAG - 1 < ALL_TILES:
-                add_bias_and_store(step - LAG - 1)
-            if 0 <= step - 1 < ALL_TILES:
+                    if last == PROJ:
+                        nc.scalar.copy(out=bias[:, last:, :], in_=spread[:, 0 : last - first, :])
+            if 0 <= step - 1 < UNITS:
                 quantise(step - 1)
-            if GPSIMD_FIRST <= step + 2 < ALL_TILES:
-                normalise_on_gpsimd(step + 2, grouped_of[step - 1])
-            if step == 3:
+                if GPSIMD_FIRST <= step + 2 < UNITS:
+                    xn = normed.tile([P, TILES, D], BF16, name="xn")
+                    xn_of[step + 2] = xn
+                    normalise_on_gpsimd(step + 2, grouped_of[step - 1])
+            if step == 1:
+                quantise_weights(0, QK)
                 quantise_weights(QK, PROJ)
+            if 0 <= step - LAG:
+                add_bias_and_store(step - LAG)

@@ -28,10 +28,11 @@ UNITS = TOKENS // UNIT
 ALL_TILES = TOKENS // P
 BANK = 512
 EPS = 1e-6
-LEAD = 3
+LEAD = 2
+HEAD = 2
 LAG = 2
 GPSIMD_COLS = 320
-GPSIMD_FIRST = 5
+GPSIMD_FIRST = 4
 
 FLOPS = 2 * TOKENS * D * PROJ * E
 
@@ -67,7 +68,6 @@ def tile_tinyblock_pa_t_kernel(
         nc.gpsimd.memset(gain_row[:].bitcast(I32), 0)
         bias_row = const.tile([P, PROJ * E], BF16)
         nc.gpsimd.memset(bias_row[:].bitcast(I32), 0)
-        nc.sync.dma_start(out=gain_row[0:1, :], in_=attn_norm_w.unsqueeze(0))
 
         w_raw = const.tile([P, PROJ, PASSES, PACK, E], BF16)
 
@@ -85,6 +85,8 @@ def tile_tinyblock_pa_t_kernel(
             if by_tile:
                 for j in range(TILES):
                     nc.sync.dma_start(out=x_unit[:, j, :], in_=rows[:, j, :])
+                    if j == 0:
+                        nc.sync.dma_start(out=gain_row[0:1, :], in_=attn_norm_w.unsqueeze(0))
             else:
                 nc.sync.dma_start(out=x_unit[:], in_=rows)
             x_units.append(x_unit)
@@ -92,12 +94,12 @@ def tile_tinyblock_pa_t_kernel(
         load_unit(0, True)
         load_weight(0)
         load_unit(1, False)
+        load_weight(2)
         for i in range(PROJ):
             nc.sync.dma_start(
                 out=bias_row[0:1, i * E : (i + 1) * E], in_=biases[i].unsqueeze(0)
             )
-        for i in range(1, PROJ):
-            load_weight(i)
+        load_weight(1)
         for u in range(2, UNITS):
             load_unit(u, False)
 
@@ -118,7 +120,6 @@ def tile_tinyblock_pa_t_kernel(
                 out=gain_psum[:, h * BANK : (h + 1) * BANK], lhsT=ones[:],
                 rhs=gain_row[:, h * BANK : (h + 1) * BANK], start=True, stop=True,
             )
-        nc.vector.tensor_copy(out=gain_sbuf[:], in_=gain_psum[:])
         bias = const.tile([P, QK + TILES, E], F32)
         bias_psum = []
         for first, last in ((0, QK), (QK, PROJ)):
@@ -265,52 +266,61 @@ def tile_tinyblock_pa_t_kernel(
 
         def add_bias_and_store(u):
             result = store.tile([P, PROJ, TILES, E], F32, name="result")
+            rows = [
+                out_i[u * UNIT : (u + 1) * UNIT, :].rearrange("(p j) e -> p j e", j=TILES)
+                for out_i in out_rows
+            ]
+            last = u == UNITS - 1
             for j in range(TILES):
                 nc.vector.tensor_tensor(
                     out=result[:, 0:QK, j, :], in0=acc_of[u, j][:], in1=bias[:, 0:QK, :],
                     op=ALU.add,
                 )
+                if last:
+                    for i in range(QK):
+                        nc.sync.dma_start(out=rows[i][:, j, :], in_=result[:, i, j, :])
             nc.vector.tensor_tensor(
                 out=result[:, QK], in0=acc_of[u, "v"][:], in1=bias[:, QK:, :], op=ALU.add
             )
-            for i in range(PROJ):
-                nc.sync.dma_start(
-                    out=out_rows[i][u * UNIT : (u + 1) * UNIT, :].rearrange(
-                        "(p j) e -> p j e", j=TILES
-                    ),
-                    in_=result[:, i],
-                )
+            for i in range(QK if last else 0, PROJ):
+                nc.sync.dma_start(out=rows[i], in_=result[:, i])
 
         group_weight_on_gpsimd(0)
         group_weight_on_gpsimd(1)
         for j in range(TILES):
             square(0, j)
             invert(0, j, j + 1)
-        known = 1
+        squared_tiles = TILES
         for step in range(UNITS + LAG):
-            wanted = min(UNITS, step + (2 if step < 2 else 3 if step == 2 else LEAD + 1))
-            todo = list(range(known, wanted))
-            known = wanted
-            if step < UNITS:
-                if step < GPSIMD_FIRST:
-                    xn = normed.tile([P, TILES, D], BF16, name="xn")
-                    xn_of[step] = xn
+            lead = 1 if step < HEAD else LEAD
+            todo = list(range(squared_tiles, min(ALL_TILES, TILES * (step + 1 + lead))))
+            squared_tiles += len(todo)
+            if step < HEAD:
+                for n in todo:
+                    square(n // TILES, n % TILES)
+                invert(step + 1, 0, TILES)
+                todo = []
+            if step < GPSIMD_FIRST:
+                xn = normed.tile([P, TILES, D], BF16, name="xn")
+                xn_of[step] = xn
             for j in range(TILES):
                 if step < UNITS:
                     normalise_on_vector(step, j)
+                    if step == 0 and j == 0:
+                        nc.vector.tensor_copy(out=gain_sbuf[:], in_=gain_psum[:])
                 if 0 <= step - LAG:
                     project(step - LAG, j)
                 if step < UNITS:
                     transpose(step, j)
-                for u in todo[0:1]:
-                    square(u, j)
+                for n in todo[j : j + 1]:
+                    square(n // TILES, n % TILES)
                 if step < UNITS:
                     copy_out(step, j)
-            for i, u in enumerate(todo):
-                if i > 0:
-                    for j in range(TILES):
-                        square(u, j)
-                invert(u, 0, TILES)
+            for i, n in enumerate(todo):
+                if i >= TILES:
+                    square(n // TILES, n % TILES)
+                if n % TILES == TILES - 1:
+                    invert(n // TILES, 0, TILES)
             if step == 0:
                 group_weight_on_vector(2)
                 for spread, first, last in bias_psum:
@@ -319,10 +329,10 @@ def tile_tinyblock_pa_t_kernel(
                         nc.scalar.copy(out=bias[:, last:, :], in_=spread[:, 0 : last - first, :])
             if 0 <= step - 1 < UNITS:
                 quantise(step - 1)
-                if GPSIMD_FIRST <= step + 2 < UNITS:
+                if GPSIMD_FIRST <= step + 1 < UNITS:
                     xn = normed.tile([P, TILES, D], BF16, name="xn")
-                    xn_of[step + 2] = xn
-                    normalise_on_gpsimd(step + 2, grouped_of[step - 1])
+                    xn_of[step + 1] = xn
+                    normalise_on_gpsimd(step + 1, grouped_of[step - 1])
             if step == 1:
                 quantise_weights(0, QK)
                 quantise_weights(QK, PROJ)

@@ -28,10 +28,10 @@ UNITS = TOKENS // UNIT
 ALL_TILES = TOKENS // P
 BANK = 512
 EPS = 1e-6
-LEAD = 2
+LEAD = 3
 HEAD = 2
 LAG = 2
-GPSIMD_COLS = 320
+GPSIMD_COLS = 304
 GPSIMD_FIRST = 4
 
 FLOPS = 2 * TOKENS * D * PROJ * E
@@ -54,7 +54,7 @@ def tile_tinyblock_pa_t_kernel(
         ctx.enter_context(tc.manual_schedule())
         const = ctx.enter_context(tc.tile_pool(name="const", bufs=1))
         x_pool = ctx.enter_context(tc.tile_pool(name="x", bufs=UNITS))
-        small = ctx.enter_context(tc.tile_pool(name="small", bufs=LEAD + 3))
+        small = ctx.enter_context(tc.tile_pool(name="small", bufs=5))
         squared = ctx.enter_context(tc.tile_pool(name="squared", bufs=2))
         normed = ctx.enter_context(tc.tile_pool(name="normed", bufs=4))
         work = ctx.enter_context(tc.tile_pool(name="work", bufs=3))
@@ -162,8 +162,10 @@ def tile_tinyblock_pa_t_kernel(
         codes_of = {}
         scales_of = {}
         acc_of = {}
+        result_of = {}
 
-        def square(u, j):
+        def square(n):
+            u, j = divmod(n, TILES)
             if j == 0:
                 sumsq = small.tile([P, TILES], F32, name="sumsq")
                 sumsq_of[u] = sumsq
@@ -174,6 +176,10 @@ def tile_tinyblock_pa_t_kernel(
                 out=squares[:], in_=x_units[u][:, j, :], func=ACT.Square,
                 accum_out=sumsq_of[u][:, j : j + 1],
             )
+            if u == 0:
+                invert(u, j, j + 1)
+            elif j == TILES - 1:
+                invert(u, 0, TILES)
 
         def invert(u, first, last):
             nc.scalar.activation(
@@ -264,41 +270,46 @@ def tile_tinyblock_pa_t_kernel(
                 acc_of[u, "v"] = acc_v
             passes(u, j, acc_of[u, "v"][:, j, :], QK, PROJ)
 
-        def add_bias_and_store(u):
-            result = store.tile([P, PROJ, TILES, E], F32, name="result")
-            rows = [
-                out_i[u * UNIT : (u + 1) * UNIT, :].rearrange("(p j) e -> p j e", j=TILES)
-                for out_i in out_rows
-            ]
-            last = u == UNITS - 1
-            for j in range(TILES):
-                nc.vector.tensor_tensor(
-                    out=result[:, 0:QK, j, :], in0=acc_of[u, j][:], in1=bias[:, 0:QK, :],
-                    op=ALU.add,
-                )
-                if last:
-                    for i in range(QK):
-                        nc.sync.dma_start(out=rows[i][:, j, :], in_=result[:, i, j, :])
+        def rows_of(u, i):
+            return out_rows[i][u * UNIT : (u + 1) * UNIT, :].rearrange("(p j) e -> p j e", j=TILES)
+
+        def add_qk_bias(u, j):
+            if j == 0:
+                result = store.tile([P, PROJ, TILES, E], F32, name="result")
+                result_of[u] = result
             nc.vector.tensor_tensor(
-                out=result[:, QK], in0=acc_of[u, "v"][:], in1=bias[:, QK:, :], op=ALU.add
+                out=result_of[u][:, 0:QK, j, :], in0=acc_of[u, j][:], in1=bias[:, 0:QK, :],
+                op=ALU.add,
             )
-            for i in range(QK if last else 0, PROJ):
-                nc.sync.dma_start(out=rows[i], in_=result[:, i])
+            for i in range(QK):
+                if u == UNITS - 1:
+                    nc.sync.dma_start(
+                        out=rows_of(u, i)[:, j, :], in_=result_of[u][:, i, j, :]
+                    )
+                elif j == TILES - 1:
+                    nc.sync.dma_start(out=rows_of(u, i), in_=result_of[u][:, i])
+
+        def add_second_half(u):
+            add_qk_bias(u, 1)
+            add_v_bias(u)
+
+        def add_v_bias(u):
+            nc.vector.tensor_tensor(
+                out=result_of[u][:, QK], in0=acc_of[u, "v"][:], in1=bias[:, QK:, :], op=ALU.add
+            )
+            nc.sync.dma_start(out=rows_of(u, QK), in_=result_of[u][:, QK])
 
         group_weight_on_gpsimd(0)
         group_weight_on_gpsimd(1)
-        for j in range(TILES):
-            square(0, j)
-            invert(0, j, j + 1)
+        for n in range(TILES):
+            square(n)
         squared_tiles = TILES
-        for step in range(UNITS + LAG):
-            lead = 1 if step < HEAD else LEAD
-            todo = list(range(squared_tiles, min(ALL_TILES, TILES * (step + 1 + lead))))
+        for step in range(UNITS + LAG + 1):
+            todo = list(range(squared_tiles, min(ALL_TILES, TILES * (step + 1) + LEAD)))
             squared_tiles += len(todo)
             if step < HEAD:
                 for n in todo:
-                    square(n // TILES, n % TILES)
-                invert(step + 1, 0, TILES)
+                    square(n)
                 todo = []
             if step < GPSIMD_FIRST:
                 xn = normed.tile([P, TILES, D], BF16, name="xn")
@@ -308,25 +319,22 @@ def tile_tinyblock_pa_t_kernel(
                     normalise_on_vector(step, j)
                     if step == 0 and j == 0:
                         nc.vector.tensor_copy(out=gain_sbuf[:], in_=gain_psum[:])
-                if 0 <= step - LAG:
+                if 0 <= step - LAG < UNITS:
                     project(step - LAG, j)
                 if step < UNITS:
                     transpose(step, j)
                 for n in todo[j : j + 1]:
-                    square(n // TILES, n % TILES)
+                    square(n)
                 if step < UNITS:
                     copy_out(step, j)
-            for i, n in enumerate(todo):
-                if i >= TILES:
-                    square(n // TILES, n % TILES)
-                if n % TILES == TILES - 1:
-                    invert(n // TILES, 0, TILES)
             if step == 0:
                 group_weight_on_vector(2)
                 for spread, first, last in bias_psum:
                     nc.scalar.copy(out=bias[:, first:last, :], in_=spread[:, 0 : last - first, :])
                     if last == PROJ:
                         nc.scalar.copy(out=bias[:, last:, :], in_=spread[:, 0 : last - first, :])
+            if step == UNITS:
+                add_second_half(step - LAG - 1)
             if 0 <= step - 1 < UNITS:
                 quantise(step - 1)
                 if GPSIMD_FIRST <= step + 1 < UNITS:
@@ -336,5 +344,7 @@ def tile_tinyblock_pa_t_kernel(
             if step == 1:
                 quantise_weights(0, QK)
                 quantise_weights(QK, PROJ)
-            if 0 <= step - LAG:
-                add_bias_and_store(step - LAG)
+            if 0 <= step - LAG - 1 and step != UNITS:
+                add_second_half(step - LAG - 1)
+            if 0 <= step - LAG < UNITS:
+                add_qk_bias(step - LAG, 0)

@@ -31,7 +31,7 @@ EPS = 1e-6
 LEAD = 3
 HEAD = 2
 LAG = 2
-GPSIMD_COLS = 304
+GPSIMD_COLS = 320
 GPSIMD_FIRST = 4
 
 FLOPS = 2 * TOKENS * D * PROJ * E
@@ -121,14 +121,18 @@ def tile_tinyblock_pa_t_kernel(
                 rhs=gain_row[:, h * BANK : (h + 1) * BANK], start=True, stop=True,
             )
         bias = const.tile([P, QK + TILES, E], F32)
-        bias_psum = []
-        for first, last in ((0, QK), (QK, PROJ)):
-            spread = psum_o.tile([P, QK, E], F32, tag="acc", name="spread")
-            nc.tensor.matmul(
-                out=spread[:, 0 : last - first, :].rearrange("p i n -> p (i n)"), lhsT=ones[:],
-                rhs=bias_row[:, first * E : last * E], start=True, stop=True,
-            )
-            bias_psum.append((spread, first, last))
+
+        def spread_biases():
+            for first, parts in ((0, ((0, QK),)), (QK, ((QK, PROJ), (QK, PROJ)))):
+                spread = psum_o.tile([P, QK, E], F32, tag="acc", name="spread")
+                at = 0
+                for low, high in parts:
+                    nc.tensor.matmul(
+                        out=spread[:, at : at + high - low, :].rearrange("p i n -> p (i n)"),
+                        lhsT=ones[:], rhs=bias_row[:, low * E : high * E], start=True, stop=True,
+                    )
+                    at += high - low
+                nc.scalar.copy(out=bias[:, first : first + QK, :], in_=spread[:])
 
         w_grouped = const.tile([P, PASSES, PROJ, E, PACK], BF16, align_bytes=64)
         w_codes = const.tile([P, PASSES, PROJ, E], U32, align_bytes=64)
@@ -305,11 +309,13 @@ def tile_tinyblock_pa_t_kernel(
             square(n)
         squared_tiles = TILES
         for step in range(UNITS + LAG + 1):
-            todo = list(range(squared_tiles, min(ALL_TILES, TILES * (step + 1) + LEAD)))
+            lead = TILES if step == 0 else LEAD
+            todo = list(range(squared_tiles, min(ALL_TILES, TILES * (step + 1) + lead)))
             squared_tiles += len(todo)
             if step < HEAD:
-                for n in todo:
+                for n in todo[0:TILES]:
                     square(n)
+                rest = todo[TILES:]
                 todo = []
             if step < GPSIMD_FIRST:
                 xn = normed.tile([P, TILES, D], BF16, name="xn")
@@ -329,10 +335,10 @@ def tile_tinyblock_pa_t_kernel(
                     copy_out(step, j)
             if step == 0:
                 group_weight_on_vector(2)
-                for spread, first, last in bias_psum:
-                    nc.scalar.copy(out=bias[:, first:last, :], in_=spread[:, 0 : last - first, :])
-                    if last == PROJ:
-                        nc.scalar.copy(out=bias[:, last:, :], in_=spread[:, 0 : last - first, :])
+            if step == 1:
+                spread_biases()
+                for n in rest:
+                    square(n)
             if step == UNITS:
                 add_second_half(step - LAG - 1)
             if 0 <= step - 1 < UNITS:

@@ -31,7 +31,7 @@ EPS = 1e-6
 LEAD = 3
 HEAD = 2
 LAG = 2
-GPSIMD_COLS = 320
+GPSIMD_COLS = 304
 GPSIMD_FIRST = 4
 
 FLOPS = 2 * TOKENS * D * PROJ * E

from contextlib import ExitStack

import concourse.mybir as mybir
from concourse.masks import make_identity

F32 = mybir.dt.float32
BF16 = mybir.dt.bfloat16
I32 = mybir.dt.int32
U32 = mybir.dt.uint32
U8 = mybir.dt.uint8
FP8X4 = mybir.dt.float8_e4m3fn_x4
ACT = mybir.ActivationFunctionType
ALU = mybir.AluOpType

P = 128
PACK = 4
PAIR = 2
K_PASS = P * PACK
TOKENS = 4 * 1024
D = 1024
E = 256
PROJ = 3
QK = 2
PASSES = D // K_PASS
TILES = 2
UNIT = TILES * P
UNITS = TOKENS // UNIT
ALL_TILES = TOKENS // P
BANK = 512
EPS = 1e-6
LEAD = 3
HEAD = 2
LAG = 2
GPSIMD_COLS = 304
GPSIMD_FIRST = 4

FLOPS = 2 * TOKENS * D * PROJ * E


def vector_cols(u):
    return D - GPSIMD_COLS if u >= GPSIMD_FIRST else D


def tile_tinyblock_pa_t_kernel(
    tc, x, attn_norm_w, wq, bq, wk, bk, wv, bv, out_0, out_1, out_2
):
    nc = tc.nc
    x_rows = x.flatten_outer_dims()
    out_rows = [out_0.flatten_outer_dims(), out_1.flatten_outer_dims(), out_2.flatten_outer_dims()]
    weights = [wq, wk, wv]
    biases = [bq, bk, bv]

    with ExitStack() as ctx:
        ctx.enter_context(tc.manual_schedule())
        const = ctx.enter_context(tc.tile_pool(name="const", bufs=1))
        x_pool = ctx.enter_context(tc.tile_pool(name="x", bufs=UNITS))
        small = ctx.enter_context(tc.tile_pool(name="small", bufs=5))
        squared = ctx.enter_context(tc.tile_pool(name="squared", bufs=2))
        normed = ctx.enter_context(tc.tile_pool(name="normed", bufs=4))
        work = ctx.enter_context(tc.tile_pool(name="work", bufs=3))
        coded = ctx.enter_context(tc.tile_pool(name="coded", bufs=LAG + 1))
        store = ctx.enter_context(tc.tile_pool(name="store", bufs=3))
        psum_g = ctx.enter_context(tc.psum_pool(name="psum_g", bufs=1))
        psum_t = ctx.enter_context(tc.psum_pool(name="psum_t", bufs=2))
        psum_o = ctx.enter_context(tc.psum_pool(name="psum_o", bufs=5))

        gain_row = const.tile([P, D], BF16)
        nc.gpsimd.memset(gain_row[:].bitcast(I32), 0)
        bias_row = const.tile([P, PROJ * E], BF16)
        nc.gpsimd.memset(bias_row[:].bitcast(I32), 0)

        w_raw = const.tile([P, PROJ, PASSES, PACK, E], BF16)

        def load_weight(i):
            nc.sync.dma_start(
                out=w_raw[:, i].rearrange("p c t n -> p c (t n)"),
                in_=weights[i].rearrange("(c p t) n -> p c (t n)", p=P, t=PACK),
            )

        x_units = []

        def load_unit(u, by_tile):
            x_unit = x_pool.tile([P, TILES, D], BF16, name="x_unit")
            rows = x_rows[u * UNIT : (u + 1) * UNIT, :].rearrange("(p j) f -> p j f", j=TILES)
            if by_tile:
                for j in range(TILES):
                    nc.sync.dma_start(out=x_unit[:, j, :], in_=rows[:, j, :])
                    if j == 0:
                        nc.sync.dma_start(out=gain_row[0:1, :], in_=attn_norm_w.unsqueeze(0))
            else:
                nc.sync.dma_start(out=x_unit[:], in_=rows)
            x_units.append(x_unit)

        load_unit(0, True)
        load_weight(0)
        load_unit(1, False)
        load_weight(2)
        for i in range(PROJ):
            nc.sync.dma_start(
                out=bias_row[0:1, i * E : (i + 1) * E], in_=biases[i].unsqueeze(0)
            )
        load_weight(1)
        for u in range(2, UNITS):
            load_unit(u, False)

        eps = const.tile([P, 1], F32)
        nc.vector.memset(eps[:], EPS)
        ones = const.tile([P, P], BF16)
        nc.vector.memset(ones[:], 1.0)
        ident = const.tile([P, P], F32)
        make_identity(nc, ident[:])

        warm = const.tile([P, 1], F32)
        nc.scalar.activation(out=warm[:], in_=eps[:], func=ACT.Abs_reciprocal_sqrt)

        gain_psum = psum_g.tile([P, D], BF16)
        gain_sbuf = const.tile([P, D], BF16)
        for h in range(D // BANK):
            nc.tensor.matmul(
                out=gain_psum[:, h * BANK : (h + 1) * BANK], lhsT=ones[:],
                rhs=gain_row[:, h * BANK : (h + 1) * BANK], start=True, stop=True,
            )
        bias = const.tile([P, QK + TILES, E], F32)

        def spread_biases():
            for first, parts in ((0, ((0, QK),)), (QK, ((QK, PROJ), (QK, PROJ)))):
                spread = psum_o.tile([P, QK, E], F32, tag="acc", name="spread")
                at = 0
                for low, high in parts:
                    nc.tensor.matmul(
                        out=spread[:, at : at + high - low, :].rearrange("p i n -> p (i n)"),
                        lhsT=ones[:], rhs=bias_row[:, low * E : high * E], start=True, stop=True,
                    )
                    at += high - low
                nc.scalar.copy(out=bias[:, first : first + QK, :], in_=spread[:])

        w_grouped = const.tile([P, PASSES, PROJ, E, PACK], BF16, align_bytes=64)
        w_codes = const.tile([P, PASSES, PROJ, E], U32, align_bytes=64)
        w_scales = const.tile([P, PASSES, PROJ, E], U8, align_bytes=64)

        def group_weight_on_vector(i):
            nc.vector.tensor_copy(
                out=w_grouped[:, :, i], in_=w_raw[:, i].rearrange("p c t n -> p c n t")
            )

        def group_weight_on_gpsimd(i):
            for c in range(PASSES):
                nc.gpsimd.tensor_scalar(
                    out=w_grouped[:, c, i], in0=w_raw[:, i, c].rearrange("p t n -> p n t"),
                    scalar1=1.0, scalar2=0.0, op0=ALU.mult, op1=ALU.add,
                )

        def quantise_weights(first, last):
            for c in range(PASSES):
                nc.vector.quantize_mx(
                    out=w_codes[:, c, first:last].rearrange("p i n -> p (i n)").bitcast(FP8X4),
                    scales=w_scales[:, c, first:last].rearrange("p i n -> p (i n)"),
                    in_=w_grouped[:, c, first:last].rearrange("p i n t -> p (i n t)"),
                )

        sumsq_of = {}
        rinv_of = {}
        xn_of = {}
        xt_of = {}
        grouped_of = {}
        codes_of = {}
        scales_of = {}
        acc_of = {}
        result_of = {}

        def square(n):
            u, j = divmod(n, TILES)
            if j == 0:
                sumsq = small.tile([P, TILES], F32, name="sumsq")
                sumsq_of[u] = sumsq
                rinv = small.tile([P, TILES], F32, name="rinv")
                rinv_of[u] = rinv
            squares = squared.tile([P, D], BF16, name="squares")
            nc.scalar.activation(
                out=squares[:], in_=x_units[u][:, j, :], func=ACT.Square,
                accum_out=sumsq_of[u][:, j : j + 1],
            )
            if u == 0:
                invert(u, j, j + 1)
            elif j == TILES - 1:
                invert(u, 0, TILES)

        def invert(u, first, last):
            nc.scalar.activation(
                out=rinv_of[u][:, first:last], in_=sumsq_of[u][:, first:last],
                func=ACT.Abs_reciprocal_sqrt, scale=1.0 / D, bias=eps[:],
            )

        def normalise_on_gpsimd(u, scratch):
            cols = slice(vector_cols(u), D)
            scaled = (
                scratch[:].rearrange("p j c r t -> p (j c r t)").bitcast(F32)
                [:, 0 : TILES * GPSIMD_COLS].rearrange("p (j m) -> p j m", j=TILES)
            )
            for j in range(TILES):
                nc.gpsimd.tensor_scalar(
                    out=scaled[:, j], in0=x_units[u][:, j, cols], scalar1=rinv_of[u][:, j : j + 1],
                    scalar2=1.0, op0=ALU.mult, op1=ALU.mult,
                )
            nc.gpsimd.tensor_tensor(
                out=xn_of[u][:, :, cols], in0=scaled,
                in1=gain_sbuf[:, cols].unsqueeze(1).to_broadcast([P, TILES, GPSIMD_COLS]),
                op=ALU.mult,
            )

        def normalise_on_vector(u, j):
            cols = slice(0, vector_cols(u))
            nc.vector.scalar_tensor_tensor(
                out=xn_of[u][:, j, cols], in0=x_units[u][:, j, cols],
                scalar=rinv_of[u][:, j : j + 1], in1=gain_psum[:, cols],
                op0=ALU.mult, op1=ALU.mult,
            )

        def transpose(u, j):
            xn_words = xn_of[u][:, j, :].bitcast(F32)
            xt = psum_t.tile([P, PASSES, PAIR, P], F32, name="xt")
            for c in range(PASSES):
                for h in range(PAIR):
                    nc.tensor.transpose(
                        out=xt[:, c, h, :],
                        in_=xn_words[:, c * PAIR * P + h : (c + 1) * PAIR * P : PAIR],
                        identity=ident[:],
                    )
            xt_of[u, j] = xt

        def copy_out(u, j):
            if j == 0:
                grouped = work.tile(
                    [P, TILES, PASSES, P, PACK], BF16, name="grouped", align_bytes=64
                )
                grouped_of[u] = grouped
            nc.scalar.copy(
                out=grouped_of[u][:, j]
                .rearrange("p c r t -> p (c r t)")
                .bitcast(F32)
                .rearrange("p (c r h) -> p c r h", c=PASSES, h=PAIR),
                in_=xt_of[u, j][:].rearrange("p c h r -> p c r h"),
            )

        def quantise(u):
            codes = coded.tile([P, TILES, PASSES, P], U32, name="codes", align_bytes=64)
            scales = coded.tile([P, TILES, PASSES, P], U8, name="scales", align_bytes=64)
            nc.vector.quantize_mx(
                out=codes[:].rearrange("p j c r -> p (j c r)").bitcast(FP8X4),
                scales=scales[:].rearrange("p j c r -> p (j c r)"),
                in_=grouped_of[u][:].rearrange("p j c r t -> p (j c r t)"),
            )
            codes_of[u] = codes
            scales_of[u] = scales

        def passes(u, j, out, first, last):
            for c in range(PASSES):
                nc.tensor.matmul_mx(
                    out=out,
                    lhsT=codes_of[u][:, j, c, :].bitcast(FP8X4),
                    lhsT_scale=scales_of[u][:, j, c, :],
                    rhs=w_codes[:, c, first:last].rearrange("p i n -> p (i n)").bitcast(FP8X4),
                    rhs_scale=w_scales[:, c, first:last].rearrange("p i n -> p (i n)"),
                    start=(c == 0),
                    stop=(c == PASSES - 1),
                )

        def project(u, j):
            acc = psum_o.tile([P, QK, E], F32, tag="acc", name="acc")
            acc_of[u, j] = acc
            passes(u, j, acc[:].rearrange("p i n -> p (i n)"), 0, QK)
            if j == 0:
                acc_v = psum_o.tile([P, TILES, E], F32, tag="acc", name="acc_v")
                acc_of[u, "v"] = acc_v
            passes(u, j, acc_of[u, "v"][:, j, :], QK, PROJ)

        def rows_of(u, i):
            return out_rows[i][u * UNIT : (u + 1) * UNIT, :].rearrange("(p j) e -> p j e", j=TILES)

        def add_qk_bias(u, j):
            if j == 0:
                result = store.tile([P, PROJ, TILES, E], F32, name="result")
                result_of[u] = result
            nc.vector.tensor_tensor(
                out=result_of[u][:, 0:QK, j, :], in0=acc_of[u, j][:], in1=bias[:, 0:QK, :],
                op=ALU.add,
            )
            for i in range(QK):
                if u == UNITS - 1:
                    nc.sync.dma_start(
                        out=rows_of(u, i)[:, j, :], in_=result_of[u][:, i, j, :]
                    )
                elif j == TILES - 1:
                    nc.sync.dma_start(out=rows_of(u, i), in_=result_of[u][:, i])

        def add_second_half(u):
            add_qk_bias(u, 1)
            add_v_bias(u)

        def add_v_bias(u):
            nc.vector.tensor_tensor(
                out=result_of[u][:, QK], in0=acc_of[u, "v"][:], in1=bias[:, QK:, :], op=ALU.add
            )
            nc.sync.dma_start(out=rows_of(u, QK), in_=result_of[u][:, QK])

        group_weight_on_gpsimd(0)
        group_weight_on_gpsimd(1)
        for n in range(TILES):
            square(n)
        squared_tiles = TILES
        for step in range(UNITS + LAG + 1):
            lead = TILES if step == 0 else LEAD
            todo = list(range(squared_tiles, min(ALL_TILES, TILES * (step + 1) + lead)))
            squared_tiles += len(todo)
            if step < HEAD:
                for n in todo[0:TILES]:
                    square(n)
                rest = todo[TILES:]
                todo = []
            if step < GPSIMD_FIRST:
                xn = normed.tile([P, TILES, D], BF16, name="xn")
                xn_of[step] = xn
            for j in range(TILES):
                if step < UNITS:
                    normalise_on_vector(step, j)
                    if step == 0 and j == 0:
                        nc.vector.tensor_copy(out=gain_sbuf[:], in_=gain_psum[:])
                if 0 <= step - LAG < UNITS:
                    project(step - LAG, j)
                if step < UNITS:
                    transpose(step, j)
                for n in todo[j : j + 1]:
                    square(n)
                if step < UNITS:
                    copy_out(step, j)
            if step == 0:
                group_weight_on_vector(2)
            if step == 1:
                spread_biases()
                for n in rest:
                    square(n)
            if step == UNITS:
                add_second_half(step - LAG - 1)
            if 0 <= step - 1 < UNITS:
                quantise(step - 1)
                if GPSIMD_FIRST <= step + 1 < UNITS:
                    xn = normed.tile([P, TILES, D], BF16, name="xn")
                    xn_of[step + 1] = xn
                    normalise_on_gpsimd(step + 1, grouped_of[step - 1])
            if step == 1:
                quantise_weights(0, QK)
                quantise_weights(QK, PROJ)
            if 0 <= step - LAG - 1 and step != UNITS:
                add_second_half(step - LAG - 1)
            if 0 <= step - LAG < UNITS:
                add_qk_bias(step - LAG, 0)
